import numpy as np
import ml_dtypes


def mxq(x, axis, fmt="e4m3"):
    dtype, down = {"e4m3": (ml_dtypes.float8_e4m3fn, 7), "e5m2": (ml_dtypes.float8_e5m2, 14)}[fmt]
    v = np.moveaxis(np.asarray(x, np.float32).astype(ml_dtypes.bfloat16).astype(np.float64), axis, -1)
    blocks = v.reshape(v.shape[:-1] + (-1, 32))
    amax = np.abs(blocks).max(-1, keepdims=True)
    byte = np.maximum(np.where(amax > 0, np.frexp(amax)[1] - 1 + 127, 0) - down, 1)
    scale = np.exp2(byte - 127.0)
    codes = (blocks / scale).astype(np.float32).astype(dtype).astype(np.float64)
    return np.moveaxis((codes * scale).reshape(v.shape), -1, axis)


WIDE = False


def mx_kscale(k):
    if not WIDE:
        return np.ones(k)
    levels = np.array([10, -10, 5, -5, 0])
    a = np.random.permutation(np.resize(levels, k // 512 * 4)).reshape(k // 512, 4)
    idx = np.arange(k)
    return np.exp2(a[idx // 512, idx % 128 // 32])


BF16 = ml_dtypes.bfloat16


def bf(x):
    return np.asarray(x, np.float32).astype(BF16)


def f64(x):
    return np.asarray(x).astype(np.float64)


B, S, U, G, G2, N = 640, 10, 40, 512, 1024, 128


def setup_inputs():
    s, t = mx_kscale(G), mx_kscale(G2)
    e = np.exp(np.random.standard_normal((B, S)))
    return {"g1": bf(np.maximum(np.random.standard_normal((B, S, G)), 0.0) * s),
            "iab": bf(e / e.sum(1, keepdims=True)),
            "sW2": bf(np.random.standard_normal((G2, G)) * np.sqrt(2.0 / G) / s * t[:, None]),
            "sb2": bf(np.random.standard_normal(G2) * 0.3 * t),
            "sW3": bf(np.random.standard_normal((N, G2)) * 1.5 * np.sqrt(2.0 / G2) / t),
            "sb3": bf(np.random.standard_normal(N) * 0.5)}


def reference(g1, iab, sW2, sb2, sW3, sb3):
    h = np.maximum((mxq(f64(g1), 2, "e4m3") @ mxq(f64(sW2), 1, "e4m3").T) + f64(sb2), 0.0)
    z = (mxq(h, 2, "e4m3") @ mxq(f64(sW3), 1, "e4m3").T) + f64(sb3)
    e = np.exp(z - z.max(-1, keepdims=True))
    return e / e.sum(-1, keepdims=True) * f64(iab)[:, :, None]

@@ -1,0 +1,321 @@
+from contextlib import ExitStack
+
+import concourse.mybir as mybir
+from concourse.masks import make_identity
+
+F32 = mybir.dt.float32
+BF16 = mybir.dt.bfloat16
+U32 = mybir.dt.uint32
+U8 = mybir.dt.uint8
+FP8X4 = mybir.dt.float8_e4m3fn_x4
+ACT = mybir.ActivationFunctionType
+ALU = mybir.AluOpType
+AX = mybir.AxisListType
+
+P = 128
+TOKENS = 6400
+G = 512
+G2 = 1024
+NOUT = 128
+SUBS = TOKENS // P
+FLOPS = 2 * TOKENS * G * G2 + 2 * TOKENS * G2 * NOUT
+
+PINNED = False
+LOOK = 3
+
+
+def tile_resourceallocationnetwork_pa_t_kernel(tc, g1, iab, sW2, sb2, sW3, sb3, out):
+    nc = tc.nc
+    nsubs = [4] * (SUBS // 4) + ([SUBS % 4] if SUBS % 4 else [])
+    ns = len(nsubs)
+
+    g1v = g1.flatten_outer_dims().rearrange("(p i) k -> p (i k)", i=SUBS)
+    outv = out.flatten_outer_dims().rearrange("(p i) n -> p i n", i=SUBS)
+    iabv = iab.rearrange("(p q) s -> p (q s)", p=P)
+    w2v = sW2.rearrange("(g p t) k -> g p (t k)", g=2, t=4)
+    b2v = sb2.rearrange("(g p t) -> p g t", g=2, t=4)
+
+    with ExitStack() as ctx:
+        if PINNED:
+            ctx.enter_context(tc.manual_schedule())
+        const = ctx.enter_context(tc.tile_pool(name="const", bufs=1))
+        raw = ctx.enter_context(tc.tile_pool(name="raw", bufs=1))
+        keep = ctx.enter_context(tc.tile_pool(name="keep", bufs=1))
+        xgp = ctx.enter_context(tc.tile_pool(name="xgp", bufs=3))
+        hpp = ctx.enter_context(tc.tile_pool(name="hpp", bufs=3))
+        hgp = ctx.enter_context(tc.tile_pool(name="hgp", bufs=3))
+        hcp = ctx.enter_context(tc.tile_pool(name="hcp", bufs=4))
+        epp = ctx.enter_context(tc.tile_pool(name="epp", bufs=3))
+        sml = ctx.enter_context(tc.tile_pool(name="sml", bufs=4))
+        psx = ctx.enter_context(tc.psum_pool(name="psx", bufs=2))
+        psh = ctx.enter_context(tc.psum_pool(name="psh", bufs=4))
+        psz = ctx.enter_context(tc.psum_pool(name="psz", bufs=2))
+
+        ident = const.tile([P, P], F32, name="ident")
+        make_identity(nc, ident[:])
+        warm_in = const.tile([P, 1], F32, name="warm_in")
+        warm_out = const.tile([P, 1], F32, name="warm_out")
+        nc.vector.memset(warm_in[:], 0.0)
+        nc.scalar.activation(out=warm_out[:], in_=warm_in[:], func=ACT.Exp)
+
+        b2raw = const.tile([P, 2, 4], BF16, name="b2raw")
+        c3raw = const.tile([P, NOUT], BF16, name="c3raw")
+        iabraw = const.tile([P, SUBS], BF16, name="iabraw")
+        nc.scalar.dma_start(out=b2raw[:], in_=b2v)
+        nc.scalar.dma_start(out=c3raw[:], in_=sb3.partition_broadcast(P))
+        nc.scalar.dma_start(out=iabraw[:], in_=iabv)
+
+        w2raw = [raw.tile([P, 4 * G], BF16, name="w2raw%d" % g) for g in range(2)]
+        w3raw = raw.tile([P, G2], BF16, name="w3raw")
+        g1t = [raw.tile([P, nsubs[s] * G], BF16, name="g1t%d" % s) for s in range(ns)]
+
+        def load_g1(s):
+            nc.sync.dma_start(out=g1t[s][:], in_=g1v[:, 4 * G * s : 4 * G * s + nsubs[s] * G])
+
+        nc.sync.dma_start(out=w2raw[0][:], in_=w2v[0])
+        load_g1(0)
+        nc.sync.dma_start(out=w2raw[1][:], in_=w2v[1])
+        load_g1(1)
+        nc.sync.dma_start(out=w3raw[:], in_=sW3)
+        for s in range(2, ns):
+            load_g1(s)
+
+        w2c = [keep.tile([P, 512], U32, name="w2c%d" % g, align_bytes=64) for g in range(2)]
+        w2s = [keep.tile([P, 512], U8, name="w2s%d" % g, align_bytes=64) for g in range(2)]
+        w3c = keep.tile([P, 256], U32, name="w3c", align_bytes=64)
+        w3s = keep.tile([P, 256], U8, name="w3s", align_bytes=64)
+        xc = [keep.tile([P, P * nsubs[s]], U32, name="xc%d" % s, align_bytes=64) for s in range(ns)]
+        xs = [keep.tile([P, P * nsubs[s]], U8, name="xs%d" % s, align_bytes=64) for s in range(ns)]
+        b2f = const.tile([P, 8], F32, name="b2f")
+        c3f = const.tile([P, NOUT], F32, name="c3f")
+        iabf = const.tile([P, SUBS], F32, name="iabf")
+
+        banks = {}
+        grouped = {}
+
+        def words_contig(tile_ap):
+            w32 = tile_ap.bitcast(F32)
+            return lambda j, u: w32[:, 256 * j + 128 * u : 256 * j + 128 * u + 128]
+
+        def words_step2(tile_ap):
+            w32 = tile_ap.bitcast(F32)
+            return lambda j, u: w32[:, 256 * j + u : 256 * j + 256 : 2]
+
+        def xt(key, words, nsub):
+            lst = []
+            for b in range(nsub // 2):
+                xp = psx.tile([P, 2, 256], F32, name="xp")
+                for jj in range(2):
+                    for u in range(2):
+                        nc.tensor.transpose(xp[:, u, P * jj : P * jj + P], words(2 * b + jj, u), ident[:])
+                lst.append(xp)
+            banks[key] = lst
+
+        def xe(key, nsub):
+            xg = xgp.tile([P, 4 * P * 2], F32, name="xg", align_bytes=64)
+            for b, xp in enumerate(banks[key]):
+                dst = xg[:, 512 * b : 512 * b + 512].rearrange("p (w u) -> p w u", u=2)
+                src = xp[:].rearrange("p u w -> p w u")
+                if b == 0:
+                    nc.scalar.copy(out=dst, in_=src)
+                else:
+                    nc.vector.tensor_copy(out=dst, in_=src)
+            grouped[key] = xg
+
+        def xq(key, nsub, codes, scales):
+            xg = grouped[key]
+            nc.vector.quantize_mx(
+                out=codes.bitcast(FP8X4), scales=scales, in_=xg[:, : 2 * P * nsub].bitcast(BF16)
+            )
+
+        def x_t(s):
+            if 0 <= s < ns:
+                xt(("x", s), words_contig(g1t[s][:]), nsubs[s])
+
+        def x_e(s):
+            if 0 <= s < ns:
+                xe(("x", s), nsubs[s])
+
+        def x_q(s):
+            if 0 <= s < ns:
+                xq(("x", s), nsubs[s], xc[s][:], xs[s][:])
+
+        hb = {}
+        hp = {}
+        hg = {}
+        hc = {}
+        hs = {}
+        zb = {}
+        nzc = {}
+        mn = {}
+        ex = {}
+        ss = {}
+
+        def l1(s, g, t):
+            if not 0 <= s < ns:
+                return
+            w = P * nsubs[s]
+            hb_t = psh.tile([P, w], F32, name="hb")
+            nc.tensor.matmul_mx(
+                out=hb_t[:],
+                lhsT=w2c[g][:, P * t : P * t + P].bitcast(FP8X4),
+                lhsT_scale=w2s[g][:, P * t : P * t + P],
+                rhs=xc[s][:].bitcast(FP8X4),
+                rhs_scale=xs[s][:],
+                start=True,
+                stop=True,
+            )
+            hb[(s, g, t)] = hb_t
+
+        def ev(s, g, t):
+            if not 0 <= s < ns:
+                return
+            w = P * nsubs[s]
+            if t == 0:
+                hp[(s, g)] = hpp.tile([P, 4, w], BF16, name="hp")
+            nc.scalar.activation(
+                out=hp[(s, g)][:, t, :],
+                in_=hb[(s, g, t)][:],
+                func=ACT.Relu,
+                bias=b2f[:, 4 * g + t : 4 * g + t + 1],
+                scale=1.0,
+            )
+
+        def rg(s, g):
+            if not 0 <= s < ns:
+                return
+            w = P * nsubs[s]
+            hg_t = hgp.tile([P, 4 * w], BF16, name="hg", align_bytes=64)
+            nc.vector.tensor_copy(
+                out=hg_t[:].rearrange("p (c i t) -> p c t i", i=4, t=4),
+                in_=hp[(s, g)][:].rearrange("p t (c i) -> p c t i", i=4),
+            )
+            hg[(s, g)] = hg_t
+
+        def hq(s, g):
+            if not 0 <= s < ns:
+                return
+            w = P * nsubs[s]
+            hc_t = hcp.tile([P, w], U32, name="hc", align_bytes=64)
+            hs_t = hcp.tile([P, w], U8, name="hs", align_bytes=64)
+            nc.vector.quantize_mx(out=hc_t[:].bitcast(FP8X4), scales=hs_t[:], in_=hg[(s, g)][:])
+            hc[(s, g)] = hc_t
+            hs[(s, g)] = hs_t
+
+        def l2(s):
+            if not 0 <= s < ns:
+                return
+            zb_t = psz.tile([P, 4, NOUT], F32, name="zb")
+            for j in range(nsubs[s]):
+                for g in range(2):
+                    nc.tensor.matmul_mx(
+                        out=zb_t[:, j, :],
+                        lhsT=hc[(s, g)][:, P * j : P * j + P].bitcast(FP8X4),
+                        lhsT_scale=hs[(s, g)][:, P * j : P * j + P],
+                        rhs=w3c[:, P * g : P * g + P].bitcast(FP8X4),
+                        rhs_scale=w3s[:, P * g : P * g + P],
+                        start=(g == 0),
+                        stop=(g == 1),
+                    )
+            zb[s] = zb_t
+
+        def ep1(s):
+            if not 0 <= s < ns:
+                return
+            n = nsubs[s]
+            nzc_t = epp.tile([P, 4, NOUT], F32, name="nzc")
+            mn_t = sml.tile([P, 4], F32, name="mn")
+            nc.vector.scalar_tensor_tensor(
+                out=nzc_t[:, :n, :],
+                in0=zb[s][:, :n, :],
+                scalar=-1.0,
+                in1=c3f[:].unsqueeze(1).to_broadcast([P, n, NOUT]),
+                op0=ALU.mult,
+                op1=ALU.subtract,
+            )
+            nc.vector.tensor_reduce(out=mn_t[:, :n], in_=nzc_t[:, :n, :], axis=AX.X, op=ALU.min)
+            nzc[s] = nzc_t
+            mn[s] = mn_t
+
+        def ep2(s):
+            if not 0 <= s < ns:
+                return
+            ex_t = epp.tile([P, 4, NOUT], F32, name="ex")
+            ss_t = sml.tile([P, 4], F32, name="ss")
+            for j in range(nsubs[s]):
+                nc.scalar.activation(
+                    out=ex_t[:, j, :],
+                    in_=nzc[s][:, j, :],
+                    func=ACT.Exp,
+                    bias=mn[s][:, j : j + 1],
+                    scale=-1.0,
+                    accum_out=ss_t[:, j : j + 1],
+                )
+            ex[s] = ex_t
+            ss[s] = ss_t
+
+        def ep3(s):
+            if not 0 <= s < ns:
+                return
+            n = nsubs[s]
+            rs_t = sml.tile([P, 4], F32, name="rs")
+            rr_t = sml.tile([P, 4], F32, name="rr")
+            ot = epp.tile([P, 4, NOUT], F32, name="ot")
+            nc.vector.reciprocal(out=rs_t[:, :n], in_=ss[s][:, :n])
+            nc.vector.tensor_tensor(
+                out=rr_t[:, :n], in0=rs_t[:, :n], in1=iabf[:, 4 * s : 4 * s + n], op=ALU.mult
+            )
+            for j in range(n):
+                nc.vector.tensor_scalar(
+                    out=ot[:, j, :], in0=ex[s][:, j, :], scalar1=rr_t[:, j : j + 1], scalar2=None, op0=ALU.mult
+                )
+            nc.sync.dma_start(out=outv[:, 4 * s : 4 * s + n, :], in_=ot[:, :n, :])
+
+        xt("w20", words_contig(w2raw[0][:]), 4)
+        xe("w20", 4)
+        x_t(0)
+        xq("w20", 4, w2c[0][:], w2s[0][:])
+        x_e(0)
+        xt("w21", words_contig(w2raw[1][:]), 4)
+        x_q(0)
+        nc.vector.tensor_copy(out=b2f[:], in_=b2raw[:].rearrange("p g t -> p (g t)"))
+        for t in range(4):
+            l1(0, 0, t)
+        xe("w21", 4)
+        x_t(1)
+        xq("w21", 4, w2c[1][:], w2s[1][:])
+        x_e(1)
+        xt("w3", words_step2(w3raw[:]), 2)
+        x_q(1)
+        xe("w3", 2)
+        x_t(2)
+        xq("w3", 2, w3c[:], w3s[:])
+        x_e(2)
+        x_t(3)
+        x_q(2)
+        nc.vector.tensor_copy(out=c3f[:], in_=c3raw[:])
+        nc.vector.tensor_copy(out=iabf[:], in_=iabraw[:])
+
+        for s in range(ns + 2):
+            ev(s, 0, 0)
+            l1(s, 1, 0)
+            ev(s, 0, 1)
+            l1(s, 1, 1)
+            rg(s - 1, 1)
+            ep3(s - 2)
+            hq(s - 1, 1)
+            l2(s - 1)
+            ev(s, 0, 2)
+            l1(s, 1, 2)
+            ev(s, 0, 3)
+            l1(s, 1, 3)
+            x_e(s + LOOK)
+            ep1(s - 1)
+            rg(s, 0)
+            for t in range(4):
+                ev(s, 1, t)
+                l1(s + 1, 0, t)
+            x_t(s + LOOK + 1)
+            x_q(s + LOOK)
+            hq(s, 0)
+            ep2(s - 1)

@@ -22,6 +22,7 @@ FLOPS = 2 * TOKENS * G * G2 + 2 * TOKENS * G2 * NOUT
 
 PINNED = False
 LOOK = 3
+LAG = 2
 
 
 def tile_resourceallocationnetwork_pa_t_kernel(tc, g1, iab, sW2, sb2, sW3, sb3, out):
@@ -42,14 +43,12 @@ def tile_resourceallocationnetwork_pa_t_kernel(tc, g1, iab, sW2, sb2, sW3, sb3, 
         raw = ctx.enter_context(tc.tile_pool(name="raw", bufs=1))
         keep = ctx.enter_context(tc.tile_pool(name="keep", bufs=1))
         xgp = ctx.enter_context(tc.tile_pool(name="xgp", bufs=3))
-        hpp = ctx.enter_context(tc.tile_pool(name="hpp", bufs=3))
+        hpp = ctx.enter_context(tc.tile_pool(name="hpp", bufs=4))
         hgp = ctx.enter_context(tc.tile_pool(name="hgp", bufs=3))
-        hcp = ctx.enter_context(tc.tile_pool(name="hcp", bufs=4))
+        hcp = ctx.enter_context(tc.tile_pool(name="hcp", bufs=6))
         epp = ctx.enter_context(tc.tile_pool(name="epp", bufs=3))
         sml = ctx.enter_context(tc.tile_pool(name="sml", bufs=4))
-        psx = ctx.enter_context(tc.psum_pool(name="psx", bufs=2))
-        psh = ctx.enter_context(tc.psum_pool(name="psh", bufs=4))
-        psz = ctx.enter_context(tc.psum_pool(name="psz", bufs=2))
+        psum = ctx.enter_context(tc.psum_pool(name="psum", bufs=1))
 
         ident = const.tile([P, P], F32, name="ident")
         make_identity(nc, ident[:])
@@ -101,44 +100,42 @@ def tile_resourceallocationnetwork_pa_t_kernel(tc, g1, iab, sW2, sb2, sW3, sb3, 
             w32 = tile_ap.bitcast(F32)
             return lambda j, u: w32[:, 256 * j + u : 256 * j + 256 : 2]
 
-        def xt(key, words, nsub):
-            lst = []
+        def xt(key, words, nsub, bank_ids):
             for b in range(nsub // 2):
-                xp = psx.tile([P, 2, 256], F32, name="xp")
+                xp = psum.tile([P, 2, 256], F32, name="xp", tag="bank%d" % bank_ids[b])
                 for jj in range(2):
                     for u in range(2):
                         nc.tensor.transpose(xp[:, u, P * jj : P * jj + P], words(2 * b + jj, u), ident[:])
-                lst.append(xp)
-            banks[key] = lst
+                banks[(key, b)] = xp
 
-        def xe(key, nsub):
-            xg = xgp.tile([P, 4 * P * 2], F32, name="xg", align_bytes=64)
-            for b, xp in enumerate(banks[key]):
-                dst = xg[:, 512 * b : 512 * b + 512].rearrange("p (w u) -> p w u", u=2)
-                src = xp[:].rearrange("p u w -> p w u")
-                if b == 0:
-                    nc.scalar.copy(out=dst, in_=src)
-                else:
-                    nc.vector.tensor_copy(out=dst, in_=src)
-            grouped[key] = xg
+        def xe(key, b, on_scalar):
+            if b == 0:
+                grouped[key] = xgp.tile([P, 4 * P * 2], F32, name="xg", align_bytes=64)
+            dst = grouped[key][:, 512 * b : 512 * b + 512].rearrange("p (w u) -> p w u", u=2)
+            src = banks[(key, b)][:].rearrange("p u w -> p w u")
+            if on_scalar:
+                nc.scalar.copy(out=dst, in_=src)
+            else:
+                nc.vector.tensor_copy(out=dst, in_=src)
 
         def xq(key, nsub, codes, scales):
-            xg = grouped[key]
             nc.vector.quantize_mx(
-                out=codes.bitcast(FP8X4), scales=scales, in_=xg[:, : 2 * P * nsub].bitcast(BF16)
+                out=codes.bitcast(FP8X4), scales=scales, in_=grouped[key][:, : 2 * P * nsub].bitcast(BF16)
             )
 
-        def x_t(s):
+        def x_t(s, bank_ids):
             if 0 <= s < ns:
-                xt(("x", s), words_contig(g1t[s][:]), nsubs[s])
+                xt(s, words_contig(g1t[s][:]), nsubs[s], bank_ids)
 
-        def x_e(s):
+        def x_e(s, second_on_scalar):
             if 0 <= s < ns:
-                xe(("x", s), nsubs[s])
+                xe(s, 0, True)
+                if nsubs[s] == 4:
+                    xe(s, 1, second_on_scalar)
 
         def x_q(s):
             if 0 <= s < ns:
-                xq(("x", s), nsubs[s], xc[s][:], xs[s][:])
+                xq(s, nsubs[s], xc[s][:], xs[s][:])
 
         hb = {}
         hp = {}
@@ -155,7 +152,7 @@ def tile_resourceallocationnetwork_pa_t_kernel(tc, g1, iab, sW2, sb2, sW3, sb3, 
             if not 0 <= s < ns:
                 return
             w = P * nsubs[s]
-            hb_t = psh.tile([P, w], F32, name="hb")
+            hb_t = psum.tile([P, w], F32, name="hb", tag="bank%d" % (4 + t))
             nc.tensor.matmul_mx(
                 out=hb_t[:],
                 lhsT=w2c[g][:, P * t : P * t + P].bitcast(FP8X4),
@@ -205,7 +202,7 @@ def tile_resourceallocationnetwork_pa_t_kernel(tc, g1, iab, sW2, sb2, sW3, sb3, 
         def l2(s):
             if not 0 <= s < ns:
                 return
-            zb_t = psz.tile([P, 4, NOUT], F32, name="zb")
+            zb_t = psum.tile([P, 4, NOUT], F32, name="zb", tag="bank%d" % (2 + s % 2))
             for j in range(nsubs[s]):
                 for g in range(2):
                     nc.tensor.matmul_mx(
@@ -271,51 +268,59 @@ def tile_resourceallocationnetwork_pa_t_kernel(tc, g1, iab, sW2, sb2, sW3, sb3, 
                 )
             nc.sync.dma_start(out=outv[:, 4 * s : 4 * s + n, :], in_=ot[:, :n, :])
 
-        xt("w20", words_contig(w2raw[0][:]), 4)
-        xe("w20", 4)
-        x_t(0)
+        xt("w20", words_contig(w2raw[0][:]), 4, [4, 5])
+        x_t(0, [6, 7])
+        xt("w21", words_contig(w2raw[1][:]), 4, [0, 1])
+        x_t(1, [2, 3])
+        xe("w20", 0, True)
+        xe("w20", 1, False)
         xq("w20", 4, w2c[0][:], w2s[0][:])
-        x_e(0)
-        xt("w21", words_contig(w2raw[1][:]), 4)
+        x_e(0, False)
         x_q(0)
         nc.vector.tensor_copy(out=b2f[:], in_=b2raw[:].rearrange("p g t -> p (g t)"))
         for t in range(4):
             l1(0, 0, t)
-        xe("w21", 4)
-        x_t(1)
+        xe("w21", 0, True)
+        xe("w21", 1, False)
+        xt("w3", words_step2(w3raw[:]), 2, [0])
         xq("w21", 4, w2c[1][:], w2s[1][:])
-        x_e(1)
-        xt("w3", words_step2(w3raw[:]), 2)
+        x_e(1, False)
         x_q(1)
-        xe("w3", 2)
-        x_t(2)
+        xe("w3", 0, False)
+        x_t(2, [1, 2])
         xq("w3", 2, w3c[:], w3s[:])
-        x_e(2)
-        x_t(3)
-        x_q(2)
+        xe(2, 0, False)
+        xe(2, 1, False)
+        x_t(3, [3, 0])
         nc.vector.tensor_copy(out=c3f[:], in_=c3raw[:])
         nc.vector.tensor_copy(out=iabf[:], in_=iabraw[:])
 
-        for s in range(ns + 2):
-            ev(s, 0, 0)
-            l1(s, 1, 0)
-            ev(s, 0, 1)
-            l1(s, 1, 1)
+        for s in range(ns):
             rg(s - 1, 1)
-            ep3(s - 2)
+            ep3(s - LAG - 1)
             hq(s - 1, 1)
+            for t in range(4):
+                ev(s, 0, t)
+                l1(s, 1, t)
             l2(s - 1)
-            ev(s, 0, 2)
-            l1(s, 1, 2)
-            ev(s, 0, 3)
-            l1(s, 1, 3)
-            x_e(s + LOOK)
-            ep1(s - 1)
+            x_e(s + LOOK, True)
+            ep1(s - LAG)
+            x_q(s + LOOK - 1)
             rg(s, 0)
             for t in range(4):
                 ev(s, 1, t)
                 l1(s + 1, 0, t)
-            x_t(s + LOOK + 1)
-            x_q(s + LOOK)
             hq(s, 0)
-            ep2(s - 1)
+            x_t(s + LOOK + 1, [0, 1])
+            ep2(s - LAG)
+
+        rg(ns - 1, 1)
+        hq(ns - 1, 1)
+        l2(ns - 1)
+        ep1(ns - 2)
+        ep3(ns - 3)
+        ep2(ns - 2)
+        ep1(ns - 1)
+        ep2(ns - 1)
+        ep3(ns - 2)
+        ep3(ns - 1)

@@ -303,7 +303,7 @@ def tile_resourceallocationnetwork_pa_t_kernel(tc, g1, iab, sW2, sb2, sW3, sb3, 
                 ev(s, 0, t)
                 l1(s, 1, t)
             l2(s - 1)
-            x_e(s + LOOK, True)
+            x_e(s + LOOK, False)
             ep1(s - LAG)
             x_q(s + LOOK - 1)
             rg(s, 0)

@@ -20,7 +20,7 @@ NOUT = 128
 SUBS = TOKENS // P
 FLOPS = 2 * TOKENS * G * G2 + 2 * TOKENS * G2 * NOUT
 
-PINNED = False
+PINNED = True
 LOOK = 3
 LAG = 2
 
@@ -42,7 +42,7 @@ def tile_resourceallocationnetwork_pa_t_kernel(tc, g1, iab, sW2, sb2, sW3, sb3, 
         const = ctx.enter_context(tc.tile_pool(name="const", bufs=1))
         raw = ctx.enter_context(tc.tile_pool(name="raw", bufs=1))
         keep = ctx.enter_context(tc.tile_pool(name="keep", bufs=1))
-        xgp = ctx.enter_context(tc.tile_pool(name="xgp", bufs=3))
+        xgp = ctx.enter_context(tc.tile_pool(name="xgp", bufs=5))
         hpp = ctx.enter_context(tc.tile_pool(name="hpp", bufs=4))
         hgp = ctx.enter_context(tc.tile_pool(name="hgp", bufs=3))
         hcp = ctx.enter_context(tc.tile_pool(name="hcp", bufs=6))
@@ -147,6 +147,7 @@ def tile_resourceallocationnetwork_pa_t_kernel(tc, g1, iab, sW2, sb2, sW3, sb3, 
         mn = {}
         ex = {}
         ss = {}
+        rs = {}
 
         def l1(s, g, t):
             if not 0 <= s < ns:
@@ -216,12 +217,11 @@ def tile_resourceallocationnetwork_pa_t_kernel(tc, g1, iab, sW2, sb2, sW3, sb3, 
                     )
             zb[s] = zb_t
 
-        def ep1(s):
+        def stt(s):
             if not 0 <= s < ns:
                 return
             n = nsubs[s]
             nzc_t = epp.tile([P, 4, NOUT], F32, name="nzc")
-            mn_t = sml.tile([P, 4], F32, name="mn")
             nc.vector.scalar_tensor_tensor(
                 out=nzc_t[:, :n, :],
                 in0=zb[s][:, :n, :],
@@ -230,8 +230,14 @@ def tile_resourceallocationnetwork_pa_t_kernel(tc, g1, iab, sW2, sb2, sW3, sb3, 
                 op0=ALU.mult,
                 op1=ALU.subtract,
             )
-            nc.vector.tensor_reduce(out=mn_t[:, :n], in_=nzc_t[:, :n, :], axis=AX.X, op=ALU.min)
             nzc[s] = nzc_t
+
+        def mnr(s):
+            if not 0 <= s < ns:
+                return
+            n = nsubs[s]
+            mn_t = sml.tile([P, 4], F32, name="mn")
+            nc.vector.tensor_reduce(out=mn_t[:, :n], in_=nzc[s][:, :n, :], axis=AX.X, op=ALU.min)
             mn[s] = mn_t
 
         def ep2(s):
@@ -251,20 +257,27 @@ def tile_resourceallocationnetwork_pa_t_kernel(tc, g1, iab, sW2, sb2, sW3, sb3, 
             ex[s] = ex_t
             ss[s] = ss_t
 
-        def ep3(s):
+        def rc(s):
             if not 0 <= s < ns:
                 return
             n = nsubs[s]
             rs_t = sml.tile([P, 4], F32, name="rs")
-            rr_t = sml.tile([P, 4], F32, name="rr")
-            ot = epp.tile([P, 4, NOUT], F32, name="ot")
             nc.vector.reciprocal(out=rs_t[:, :n], in_=ss[s][:, :n])
-            nc.vector.tensor_tensor(
-                out=rr_t[:, :n], in0=rs_t[:, :n], in1=iabf[:, 4 * s : 4 * s + n], op=ALU.mult
-            )
+            rs[s] = rs_t
+
+        def ts(s):
+            if not 0 <= s < ns:
+                return
+            n = nsubs[s]
+            ot = epp.tile([P, 4, NOUT], F32, name="ot")
             for j in range(n):
                 nc.vector.tensor_scalar(
-                    out=ot[:, j, :], in0=ex[s][:, j, :], scalar1=rr_t[:, j : j + 1], scalar2=None, op0=ALU.mult
+                    out=ot[:, j, :],
+                    in0=ex[s][:, j, :],
+                    scalar1=rs[s][:, j : j + 1],
+                    scalar2=iabf[:, 4 * s + j : 4 * s + j + 1],
+                    op0=ALU.mult,
+                    op1=ALU.mult,
                 )
             nc.sync.dma_start(out=outv[:, 4 * s : 4 * s + n, :], in_=ot[:, :n, :])
 
@@ -274,22 +287,24 @@ def tile_resourceallocationnetwork_pa_t_kernel(tc, g1, iab, sW2, sb2, sW3, sb3, 
         x_t(1, [2, 3])
         xe("w20", 0, True)
         xe("w20", 1, False)
+        xe(0, 0, True)
+        xe(0, 1, False)
         xq("w20", 4, w2c[0][:], w2s[0][:])
-        x_e(0, False)
+        xe("w21", 0, True)
+        xe("w21", 1, False)
         x_q(0)
         nc.vector.tensor_copy(out=b2f[:], in_=b2raw[:].rearrange("p g t -> p (g t)"))
         for t in range(4):
             l1(0, 0, t)
-        xe("w21", 0, True)
-        xe("w21", 1, False)
         xt("w3", words_step2(w3raw[:]), 2, [0])
+        xe(1, 0, True)
+        xe(1, 1, False)
         xq("w21", 4, w2c[1][:], w2s[1][:])
-        x_e(1, False)
-        x_q(1)
-        xe("w3", 0, False)
         x_t(2, [1, 2])
-        xq("w3", 2, w3c[:], w3s[:])
+        xe("w3", 0, False)
+        x_q(1)
         xe(2, 0, False)
+        xq("w3", 2, w3c[:], w3s[:])
         xe(2, 1, False)
         x_t(3, [3, 0])
         nc.vector.tensor_copy(out=c3f[:], in_=c3raw[:])
@@ -297,30 +312,37 @@ def tile_resourceallocationnetwork_pa_t_kernel(tc, g1, iab, sW2, sb2, sW3, sb3, 
 
         for s in range(ns):
             rg(s - 1, 1)
-            ep3(s - LAG - 1)
+            rc(s - 3)
+            stt(s - 2)
             hq(s - 1, 1)
+            ts(s - 3)
+            mnr(s - 2)
             for t in range(4):
                 ev(s, 0, t)
                 l1(s, 1, t)
             l2(s - 1)
-            x_e(s + LOOK, False)
-            ep1(s - LAG)
-            x_q(s + LOOK - 1)
+            x_e(s + LOOK, (s + LOOK) % 3 == 0)
             rg(s, 0)
+            x_q(s + LOOK - 1)
+            hq(s, 0)
             for t in range(4):
                 ev(s, 1, t)
                 l1(s + 1, 0, t)
-            hq(s, 0)
             x_t(s + LOOK + 1, [0, 1])
-            ep2(s - LAG)
+            ep2(s - 2)
 
         rg(ns - 1, 1)
+        stt(ns - 2)
         hq(ns - 1, 1)
+        mnr(ns - 2)
         l2(ns - 1)
-        ep1(ns - 2)
-        ep3(ns - 3)
+        rc(ns - 3)
         ep2(ns - 2)
-        ep1(ns - 1)
+        ts(ns - 3)
+        stt(ns - 1)
+        rc(ns - 2)
+        mnr(ns - 1)
+        ts(ns - 2)
         ep2(ns - 1)
-        ep3(ns - 2)
-        ep3(ns - 1)
+        rc(ns - 1)
+        ts(ns - 1)

@@ -21,8 +21,8 @@ SUBS = TOKENS // P
 FLOPS = 2 * TOKENS * G * G2 + 2 * TOKENS * G2 * NOUT
 
 PINNED = True
-LOOK = 3
-LAG = 2
+LOOK = 2
+HOLD = 4
 
 
 def tile_resourceallocationnetwork_pa_t_kernel(tc, g1, iab, sW2, sb2, sW3, sb3, out):
@@ -46,8 +46,8 @@ def tile_resourceallocationnetwork_pa_t_kernel(tc, g1, iab, sW2, sb2, sW3, sb3, 
         hpp = ctx.enter_context(tc.tile_pool(name="hpp", bufs=4))
         hgp = ctx.enter_context(tc.tile_pool(name="hgp", bufs=3))
         hcp = ctx.enter_context(tc.tile_pool(name="hcp", bufs=6))
-        epp = ctx.enter_context(tc.tile_pool(name="epp", bufs=3))
-        sml = ctx.enter_context(tc.tile_pool(name="sml", bufs=4))
+        epp = ctx.enter_context(tc.tile_pool(name="epp", bufs=8))
+        sml = ctx.enter_context(tc.tile_pool(name="sml", bufs=8))
         psum = ctx.enter_context(tc.psum_pool(name="psum", bufs=1))
 
         ident = const.tile([P, P], F32, name="ident")
@@ -284,65 +284,76 @@ def tile_resourceallocationnetwork_pa_t_kernel(tc, g1, iab, sW2, sb2, sW3, sb3, 
         xt("w20", words_contig(w2raw[0][:]), 4, [4, 5])
         x_t(0, [6, 7])
         xt("w21", words_contig(w2raw[1][:]), 4, [0, 1])
-        x_t(1, [2, 3])
         xe("w20", 0, True)
         xe("w20", 1, False)
+        xq("w20", 4, w2c[0][:], w2s[0][:])
         xe(0, 0, True)
         xe(0, 1, False)
-        xq("w20", 4, w2c[0][:], w2s[0][:])
-        xe("w21", 0, True)
-        xe("w21", 1, False)
-        x_q(0)
         nc.vector.tensor_copy(out=b2f[:], in_=b2raw[:].rearrange("p g t -> p (g t)"))
-        for t in range(4):
-            l1(0, 0, t)
-        xt("w3", words_step2(w3raw[:]), 2, [0])
-        xe(1, 0, True)
-        xe(1, 1, False)
-        xq("w21", 4, w2c[1][:], w2s[1][:])
-        x_t(2, [1, 2])
-        xe("w3", 0, False)
-        x_q(1)
-        xe(2, 0, False)
-        xq("w3", 2, w3c[:], w3s[:])
-        xe(2, 1, False)
-        x_t(3, [3, 0])
         nc.vector.tensor_copy(out=c3f[:], in_=c3raw[:])
         nc.vector.tensor_copy(out=iabf[:], in_=iabraw[:])
+        x_q(0)
+        for t in range(4):
+            l1(0, 0, t)
+        xe("w21", 0, True)
+        xe("w21", 1, False)
+        x_t(1, [2, 3])
+        xt("w3", words_step2(w3raw[:]), 2, [0])
+        xe(1, 0, False)
+        xq("w21", 4, w2c[1][:], w2s[1][:])
+        xe(1, 1, False)
+        xe("w3", 0, False)
+        x_t(2, [1, 2])
 
+        last_exp = ns - 3 - HOLD
         for s in range(ns):
             rg(s - 1, 1)
-            rc(s - 3)
+            if s - 3 <= last_exp:
+                rc(s - 3)
             stt(s - 2)
             hq(s - 1, 1)
-            ts(s - 3)
+            if s - 3 <= last_exp:
+                ts(s - 3)
             mnr(s - 2)
+            if s == 0:
+                x_q(1)
+                xq("w3", 2, w3c[:], w3s[:])
             for t in range(4):
                 ev(s, 0, t)
                 l1(s, 1, t)
             l2(s - 1)
-            x_e(s + LOOK, (s + LOOK) % 3 == 0)
+            x_e(s + LOOK, False)
             rg(s, 0)
-            x_q(s + LOOK - 1)
+            if s > 0:
+                x_q(s + LOOK - 1)
             hq(s, 0)
             for t in range(4):
                 ev(s, 1, t)
                 l1(s + 1, 0, t)
             x_t(s + LOOK + 1, [0, 1])
-            ep2(s - 2)
+            if s - 2 <= last_exp:
+                ep2(s - 2)
 
+        held = list(range(last_exp + 1, ns - 2))
+        for x in held:
+            ep2(x)
         rg(ns - 1, 1)
         stt(ns - 2)
         hq(ns - 1, 1)
         mnr(ns - 2)
         l2(ns - 1)
-        rc(ns - 3)
         ep2(ns - 2)
-        ts(ns - 3)
-        stt(ns - 1)
+        rc(held[0])
+        for i, x in enumerate(held):
+            if i + 1 < len(held):
+                rc(held[i + 1])
+            ts(x)
+            if i == min(1, len(held) - 1):
+                stt(ns - 1)
+            if i == min(2, len(held) - 1):
+                mnr(ns - 1)
+                ep2(ns - 1)
         rc(ns - 2)
-        mnr(ns - 1)
-        ts(ns - 2)
-        ep2(ns - 1)
         rc(ns - 1)
+        ts(ns - 2)
         ts(ns - 1)

@@ -20,9 +20,9 @@ NOUT = 128
 SUBS = TOKENS // P
 FLOPS = 2 * TOKENS * G * G2 + 2 * TOKENS * G2 * NOUT
 
-PINNED = True
-LOOK = 2
-HOLD = 4
+PINNED = False
+LOOK = 3
+LAG = 2
 
 
 def tile_resourceallocationnetwork_pa_t_kernel(tc, g1, iab, sW2, sb2, sW3, sb3, out):
@@ -46,8 +46,8 @@ def tile_resourceallocationnetwork_pa_t_kernel(tc, g1, iab, sW2, sb2, sW3, sb3, 
         hpp = ctx.enter_context(tc.tile_pool(name="hpp", bufs=4))
         hgp = ctx.enter_context(tc.tile_pool(name="hgp", bufs=3))
         hcp = ctx.enter_context(tc.tile_pool(name="hcp", bufs=6))
-        epp = ctx.enter_context(tc.tile_pool(name="epp", bufs=8))
-        sml = ctx.enter_context(tc.tile_pool(name="sml", bufs=8))
+        epp = ctx.enter_context(tc.tile_pool(name="epp", bufs=3))
+        sml = ctx.enter_context(tc.tile_pool(name="sml", bufs=4))
         psum = ctx.enter_context(tc.psum_pool(name="psum", bufs=1))
 
         ident = const.tile([P, P], F32, name="ident")
@@ -284,76 +284,65 @@ def tile_resourceallocationnetwork_pa_t_kernel(tc, g1, iab, sW2, sb2, sW3, sb3, 
         xt("w20", words_contig(w2raw[0][:]), 4, [4, 5])
         x_t(0, [6, 7])
         xt("w21", words_contig(w2raw[1][:]), 4, [0, 1])
+        x_t(1, [2, 3])
         xe("w20", 0, True)
         xe("w20", 1, False)
-        xq("w20", 4, w2c[0][:], w2s[0][:])
         xe(0, 0, True)
         xe(0, 1, False)
-        nc.vector.tensor_copy(out=b2f[:], in_=b2raw[:].rearrange("p g t -> p (g t)"))
-        nc.vector.tensor_copy(out=c3f[:], in_=c3raw[:])
-        nc.vector.tensor_copy(out=iabf[:], in_=iabraw[:])
-        x_q(0)
-        for t in range(4):
-            l1(0, 0, t)
+        xq("w20", 4, w2c[0][:], w2s[0][:])
         xe("w21", 0, True)
         xe("w21", 1, False)
-        x_t(1, [2, 3])
+        x_q(0)
+        nc.vector.tensor_copy(out=b2f[:], in_=b2raw[:].rearrange("p g t -> p (g t)"))
+        for t in range(4):
+            l1(0, 0, t)
         xt("w3", words_step2(w3raw[:]), 2, [0])
-        xe(1, 0, False)
-        xq("w21", 4, w2c[1][:], w2s[1][:])
+        xe(1, 0, True)
         xe(1, 1, False)
-        xe("w3", 0, False)
+        xq("w21", 4, w2c[1][:], w2s[1][:])
         x_t(2, [1, 2])
+        xe("w3", 0, False)
+        x_q(1)
+        xe(2, 0, False)
+        xq("w3", 2, w3c[:], w3s[:])
+        xe(2, 1, False)
+        x_t(3, [3, 0])
+        nc.vector.tensor_copy(out=c3f[:], in_=c3raw[:])
+        nc.vector.tensor_copy(out=iabf[:], in_=iabraw[:])
 
-        last_exp = ns - 3 - HOLD
         for s in range(ns):
             rg(s - 1, 1)
-            if s - 3 <= last_exp:
-                rc(s - 3)
+            rc(s - 3)
             stt(s - 2)
             hq(s - 1, 1)
-            if s - 3 <= last_exp:
-                ts(s - 3)
+            ts(s - 3)
             mnr(s - 2)
-            if s == 0:
-                x_q(1)
-                xq("w3", 2, w3c[:], w3s[:])
             for t in range(4):
                 ev(s, 0, t)
                 l1(s, 1, t)
             l2(s - 1)
-            x_e(s + LOOK, False)
+            x_e(s + LOOK, (s + LOOK) % 3 == 0)
             rg(s, 0)
-            if s > 0:
-                x_q(s + LOOK - 1)
+            x_q(s + LOOK - 1)
             hq(s, 0)
             for t in range(4):
                 ev(s, 1, t)
                 l1(s + 1, 0, t)
             x_t(s + LOOK + 1, [0, 1])
-            if s - 2 <= last_exp:
-                ep2(s - 2)
+            ep2(s - 2)
 
-        held = list(range(last_exp + 1, ns - 2))
-        for x in held:
-            ep2(x)
         rg(ns - 1, 1)
         stt(ns - 2)
         hq(ns - 1, 1)
         mnr(ns - 2)
         l2(ns - 1)
+        rc(ns - 3)
         ep2(ns - 2)
-        rc(held[0])
-        for i, x in enumerate(held):
-            if i + 1 < len(held):
-                rc(held[i + 1])
-            ts(x)
-            if i == min(1, len(held) - 1):
-                stt(ns - 1)
-            if i == min(2, len(held) - 1):
-                mnr(ns - 1)
-                ep2(ns - 1)
+        ts(ns - 3)
+        stt(ns - 1)
         rc(ns - 2)
-        rc(ns - 1)
+        mnr(ns - 1)
         ts(ns - 2)
+        ep2(ns - 1)
+        rc(ns - 1)
         ts(ns - 1)

from contextlib import ExitStack

import concourse.mybir as mybir
from concourse.masks import make_identity

F32 = mybir.dt.float32
BF16 = mybir.dt.bfloat16
U32 = mybir.dt.uint32
U8 = mybir.dt.uint8
FP8X4 = mybir.dt.float8_e4m3fn_x4
ACT = mybir.ActivationFunctionType
ALU = mybir.AluOpType
AX = mybir.AxisListType

P = 128
TOKENS = 6400
G = 512
G2 = 1024
NOUT = 128
SUBS = TOKENS // P
FLOPS = 2 * TOKENS * G * G2 + 2 * TOKENS * G2 * NOUT

PINNED = False
LOOK = 3
LAG = 2


def tile_resourceallocationnetwork_pa_t_kernel(tc, g1, iab, sW2, sb2, sW3, sb3, out):
    nc = tc.nc
    nsubs = [4] * (SUBS // 4) + ([SUBS % 4] if SUBS % 4 else [])
    ns = len(nsubs)

    g1v = g1.flatten_outer_dims().rearrange("(p i) k -> p (i k)", i=SUBS)
    outv = out.flatten_outer_dims().rearrange("(p i) n -> p i n", i=SUBS)
    iabv = iab.rearrange("(p q) s -> p (q s)", p=P)
    w2v = sW2.rearrange("(g p t) k -> g p (t k)", g=2, t=4)
    b2v = sb2.rearrange("(g p t) -> p g t", g=2, t=4)

    with ExitStack() as ctx:
        if PINNED:
            ctx.enter_context(tc.manual_schedule())
        const = ctx.enter_context(tc.tile_pool(name="const", bufs=1))
        raw = ctx.enter_context(tc.tile_pool(name="raw", bufs=1))
        keep = ctx.enter_context(tc.tile_pool(name="keep", bufs=1))
        xgp = ctx.enter_context(tc.tile_pool(name="xgp", bufs=5))
        hpp = ctx.enter_context(tc.tile_pool(name="hpp", bufs=4))
        hgp = ctx.enter_context(tc.tile_pool(name="hgp", bufs=3))
        hcp = ctx.enter_context(tc.tile_pool(name="hcp", bufs=6))
        epp = ctx.enter_context(tc.tile_pool(name="epp", bufs=3))
        sml = ctx.enter_context(tc.tile_pool(name="sml", bufs=4))
        psum = ctx.enter_context(tc.psum_pool(name="psum", bufs=1))

        ident = const.tile([P, P], F32, name="ident")
        make_identity(nc, ident[:])
        warm_in = const.tile([P, 1], F32, name="warm_in")
        warm_out = const.tile([P, 1], F32, name="warm_out")
        nc.vector.memset(warm_in[:], 0.0)
        nc.scalar.activation(out=warm_out[:], in_=warm_in[:], func=ACT.Exp)

        b2raw = const.tile([P, 2, 4], BF16, name="b2raw")
        c3raw = const.tile([P, NOUT], BF16, name="c3raw")
        iabraw = const.tile([P, SUBS], BF16, name="iabraw")
        nc.scalar.dma_start(out=b2raw[:], in_=b2v)
        nc.scalar.dma_start(out=c3raw[:], in_=sb3.partition_broadcast(P))
        nc.scalar.dma_start(out=iabraw[:], in_=iabv)

        w2raw = [raw.tile([P, 4 * G], BF16, name="w2raw%d" % g) for g in range(2)]
        w3raw = raw.tile([P, G2], BF16, name="w3raw")
        g1t = [raw.tile([P, nsubs[s] * G], BF16, name="g1t%d" % s) for s in range(ns)]

        def load_g1(s):
            nc.sync.dma_start(out=g1t[s][:], in_=g1v[:, 4 * G * s : 4 * G * s + nsubs[s] * G])

        nc.sync.dma_start(out=w2raw[0][:], in_=w2v[0])
        load_g1(0)
        nc.sync.dma_start(out=w2raw[1][:], in_=w2v[1])
        load_g1(1)
        nc.sync.dma_start(out=w3raw[:], in_=sW3)
        for s in range(2, ns):
            load_g1(s)

        w2c = [keep.tile([P, 512], U32, name="w2c%d" % g, align_bytes=64) for g in range(2)]
        w2s = [keep.tile([P, 512], U8, name="w2s%d" % g, align_bytes=64) for g in range(2)]
        w3c = keep.tile([P, 256], U32, name="w3c", align_bytes=64)
        w3s = keep.tile([P, 256], U8, name="w3s", align_bytes=64)
        xc = [keep.tile([P, P * nsubs[s]], U32, name="xc%d" % s, align_bytes=64) for s in range(ns)]
        xs = [keep.tile([P, P * nsubs[s]], U8, name="xs%d" % s, align_bytes=64) for s in range(ns)]
        b2f = const.tile([P, 8], F32, name="b2f")
        c3f = const.tile([P, NOUT], F32, name="c3f")
        iabf = const.tile([P, SUBS], F32, name="iabf")

        banks = {}
        grouped = {}

        def words_contig(tile_ap):
            w32 = tile_ap.bitcast(F32)
            return lambda j, u: w32[:, 256 * j + 128 * u : 256 * j + 128 * u + 128]

        def words_step2(tile_ap):
            w32 = tile_ap.bitcast(F32)
            return lambda j, u: w32[:, 256 * j + u : 256 * j + 256 : 2]

        def xt(key, words, nsub, bank_ids):
            for b in range(nsub // 2):
                xp = psum.tile([P, 2, 256], F32, name="xp", tag="bank%d" % bank_ids[b])
                for jj in range(2):
                    for u in range(2):
                        nc.tensor.transpose(xp[:, u, P * jj : P * jj + P], words(2 * b + jj, u), ident[:])
                banks[(key, b)] = xp

        def xe(key, b, on_scalar):
            if b == 0:
                grouped[key] = xgp.tile([P, 4 * P * 2], F32, name="xg", align_bytes=64)
            dst = grouped[key][:, 512 * b : 512 * b + 512].rearrange("p (w u) -> p w u", u=2)
            src = banks[(key, b)][:].rearrange("p u w -> p w u")
            if on_scalar:
                nc.scalar.copy(out=dst, in_=src)
            else:
                nc.vector.tensor_copy(out=dst, in_=src)

        def xq(key, nsub, codes, scales):
            nc.vector.quantize_mx(
                out=codes.bitcast(FP8X4), scales=scales, in_=grouped[key][:, : 2 * P * nsub].bitcast(BF16)
            )

        def x_t(s, bank_ids):
            if 0 <= s < ns:
                xt(s, words_contig(g1t[s][:]), nsubs[s], bank_ids)

        def x_e(s, second_on_scalar):
            if 0 <= s < ns:
                xe(s, 0, True)
                if nsubs[s] == 4:
                    xe(s, 1, second_on_scalar)

        def x_q(s):
            if 0 <= s < ns:
                xq(s, nsubs[s], xc[s][:], xs[s][:])

        hb = {}
        hp = {}
        hg = {}
        hc = {}
        hs = {}
        zb = {}
        nzc = {}
        mn = {}
        ex = {}
        ss = {}
        rs = {}

        def l1(s, g, t):
            if not 0 <= s < ns:
                return
            w = P * nsubs[s]
            hb_t = psum.tile([P, w], F32, name="hb", tag="bank%d" % (4 + t))
            nc.tensor.matmul_mx(
                out=hb_t[:],
                lhsT=w2c[g][:, P * t : P * t + P].bitcast(FP8X4),
                lhsT_scale=w2s[g][:, P * t : P * t + P],
                rhs=xc[s][:].bitcast(FP8X4),
                rhs_scale=xs[s][:],
                start=True,
                stop=True,
            )
            hb[(s, g, t)] = hb_t

        def ev(s, g, t):
            if not 0 <= s < ns:
                return
            w = P * nsubs[s]
            if t == 0:
                hp[(s, g)] = hpp.tile([P, 4, w], BF16, name="hp")
            nc.scalar.activation(
                out=hp[(s, g)][:, t, :],
                in_=hb[(s, g, t)][:],
                func=ACT.Relu,
                bias=b2f[:, 4 * g + t : 4 * g + t + 1],
                scale=1.0,
            )

        def rg(s, g):
            if not 0 <= s < ns:
                return
            w = P * nsubs[s]
            hg_t = hgp.tile([P, 4 * w], BF16, name="hg", align_bytes=64)
            nc.vector.tensor_copy(
                out=hg_t[:].rearrange("p (c i t) -> p c t i", i=4, t=4),
                in_=hp[(s, g)][:].rearrange("p t (c i) -> p c t i", i=4),
            )
            hg[(s, g)] = hg_t

        def hq(s, g):
            if not 0 <= s < ns:
                return
            w = P * nsubs[s]
            hc_t = hcp.tile([P, w], U32, name="hc", align_bytes=64)
            hs_t = hcp.tile([P, w], U8, name="hs", align_bytes=64)
            nc.vector.quantize_mx(out=hc_t[:].bitcast(FP8X4), scales=hs_t[:], in_=hg[(s, g)][:])
            hc[(s, g)] = hc_t
            hs[(s, g)] = hs_t

        def l2(s):
            if not 0 <= s < ns:
                return
            zb_t = psum.tile([P, 4, NOUT], F32, name="zb", tag="bank%d" % (2 + s % 2))
            for j in range(nsubs[s]):
                for g in range(2):
                    nc.tensor.matmul_mx(
                        out=zb_t[:, j, :],
                        lhsT=hc[(s, g)][:, P * j : P * j + P].bitcast(FP8X4),
                        lhsT_scale=hs[(s, g)][:, P * j : P * j + P],
                        rhs=w3c[:, P * g : P * g + P].bitcast(FP8X4),
                        rhs_scale=w3s[:, P * g : P * g + P],
                        start=(g == 0),
                        stop=(g == 1),
                    )
            zb[s] = zb_t

        def stt(s):
            if not 0 <= s < ns:
                return
            n = nsubs[s]
            nzc_t = epp.tile([P, 4, NOUT], F32, name="nzc")
            nc.vector.scalar_tensor_tensor(
                out=nzc_t[:, :n, :],
                in0=zb[s][:, :n, :],
                scalar=-1.0,
                in1=c3f[:].unsqueeze(1).to_broadcast([P, n, NOUT]),
                op0=ALU.mult,
                op1=ALU.subtract,
            )
            nzc[s] = nzc_t

        def mnr(s):
            if not 0 <= s < ns:
                return
            n = nsubs[s]
            mn_t = sml.tile([P, 4], F32, name="mn")
            nc.vector.tensor_reduce(out=mn_t[:, :n], in_=nzc[s][:, :n, :], axis=AX.X, op=ALU.min)
            mn[s] = mn_t

        def ep2(s):
            if not 0 <= s < ns:
                return
            ex_t = epp.tile([P, 4, NOUT], F32, name="ex")
            ss_t = sml.tile([P, 4], F32, name="ss")
            for j in range(nsubs[s]):
                nc.scalar.activation(
                    out=ex_t[:, j, :],
                    in_=nzc[s][:, j, :],
                    func=ACT.Exp,
                    bias=mn[s][:, j : j + 1],
                    scale=-1.0,
                    accum_out=ss_t[:, j : j + 1],
                )
            ex[s] = ex_t
            ss[s] = ss_t

        def rc(s):
            if not 0 <= s < ns:
                return
            n = nsubs[s]
            rs_t = sml.tile([P, 4], F32, name="rs")
            nc.vector.reciprocal(out=rs_t[:, :n], in_=ss[s][:, :n])
            rs[s] = rs_t

        def ts(s):
            if not 0 <= s < ns:
                return
            n = nsubs[s]
            ot = epp.tile([P, 4, NOUT], F32, name="ot")
            for j in range(n):
                nc.vector.tensor_scalar(
                    out=ot[:, j, :],
                    in0=ex[s][:, j, :],
                    scalar1=rs[s][:, j : j + 1],
                    scalar2=iabf[:, 4 * s + j : 4 * s + j + 1],
                    op0=ALU.mult,
                    op1=ALU.mult,
                )
            nc.sync.dma_start(out=outv[:, 4 * s : 4 * s + n, :], in_=ot[:, :n, :])

        xt("w20", words_contig(w2raw[0][:]), 4, [4, 5])
        x_t(0, [6, 7])
        xt("w21", words_contig(w2raw[1][:]), 4, [0, 1])
        x_t(1, [2, 3])
        xe("w20", 0, True)
        xe("w20", 1, False)
        xe(0, 0, True)
        xe(0, 1, False)
        xq("w20", 4, w2c[0][:], w2s[0][:])
        xe("w21", 0, True)
        xe("w21", 1, False)
        x_q(0)
        nc.vector.tensor_copy(out=b2f[:], in_=b2raw[:].rearrange("p g t -> p (g t)"))
        for t in range(4):
            l1(0, 0, t)
        xt("w3", words_step2(w3raw[:]), 2, [0])
        xe(1, 0, True)
        xe(1, 1, False)
        xq("w21", 4, w2c[1][:], w2s[1][:])
        x_t(2, [1, 2])
        xe("w3", 0, False)
        x_q(1)
        xe(2, 0, False)
        xq("w3", 2, w3c[:], w3s[:])
        xe(2, 1, False)
        x_t(3, [3, 0])
        nc.vector.tensor_copy(out=c3f[:], in_=c3raw[:])
        nc.vector.tensor_copy(out=iabf[:], in_=iabraw[:])

        for s in range(ns):
            rg(s - 1, 1)
            rc(s - 3)
            stt(s - 2)
            hq(s - 1, 1)
            ts(s - 3)
            mnr(s - 2)
            for t in range(4):
                ev(s, 0, t)
                l1(s, 1, t)
            l2(s - 1)
            x_e(s + LOOK, (s + LOOK) % 3 == 0)
            rg(s, 0)
            x_q(s + LOOK - 1)
            hq(s, 0)
            for t in range(4):
                ev(s, 1, t)
                l1(s + 1, 0, t)
            x_t(s + LOOK + 1, [0, 1])
            ep2(s - 2)

        rg(ns - 1, 1)
        stt(ns - 2)
        hq(ns - 1, 1)
        mnr(ns - 2)
        l2(ns - 1)
        rc(ns - 3)
        ep2(ns - 2)
        ts(ns - 3)
        stt(ns - 1)
        rc(ns - 2)
        mnr(ns - 1)
        ts(ns - 2)
        ep2(ns - 1)
        rc(ns - 1)
        ts(ns - 1)
